import numpy as np
import ml_dtypes


def mxq(x, axis, fmt="e4m3"):
    dtype, down = {"e4m3": (ml_dtypes.float8_e4m3fn, 7), "e5m2": (ml_dtypes.float8_e5m2, 14)}[fmt]
    v = np.moveaxis(np.asarray(x, np.float32).astype(ml_dtypes.bfloat16).astype(np.float64), axis, -1)
    blocks = v.reshape(v.shape[:-1] + (-1, 32))
    amax = np.abs(blocks).max(-1, keepdims=True)
    byte = np.maximum(np.where(amax > 0, np.frexp(amax)[1] - 1 + 127, 0) - down, 1)
    scale = np.exp2(byte - 127.0)
    codes = (blocks / scale).astype(np.float32).astype(dtype).astype(np.float64)
    return np.moveaxis((codes * scale).reshape(v.shape), -1, axis)


WIDE = False


def mx_kscale(k):
    if not WIDE:
        return np.ones(k)
    levels = np.array([10, -10, 5, -5, 0])
    a = np.random.permutation(np.resize(levels, k // 512 * 4)).reshape(k // 512, 4)
    idx = np.arange(k)
    return np.exp2(a[idx // 512, idx % 128 // 32])


BF16 = ml_dtypes.bfloat16


def bf(x):
    return np.asarray(x, np.float32).astype(BF16)


def f64(x):
    return np.asarray(x).astype(np.float64)


B, D, A = 6144, 512, 128


def setup_inputs():
    s = mx_kscale(D)
    return {
        "x": bf(np.random.standard_normal((B, D)) * s),
        "saved_x": bf(np.random.standard_normal((B, D)) * s),
        "saved_a": bf(np.random.standard_normal((B, A))),
        "saved_b": bf(0.5 + np.random.random((B, A))),
        "saved_p": bf(np.random.standard_normal((B, A))),
        "time_decay": bf(np.random.standard_normal(A)),
        "time_first": bf(np.random.standard_normal(A)),
        "k_mixed": bf(np.random.random(D)),
        "v_mixed": bf(np.random.random(D)),
        "key_weight": bf(np.random.standard_normal((D, A)) / np.sqrt(D) / s[:, None]),
        "value_weight": bf(np.random.standard_normal((D, A)) / np.sqrt(D) / s[:, None]),
    }


def reference(x, saved_x, saved_a, saved_b, saved_p, time_decay, time_first, k_mixed, v_mixed, key_weight, value_weight):
    x, saved_x = f64(x), f64(saved_x)
    saved_a, saved_b, saved_p = f64(saved_a), f64(saved_b), f64(saved_p)
    time_decay, time_first = f64(time_decay), f64(time_first)
    k_mixed, v_mixed = f64(k_mixed), f64(v_mixed)
    xk = x * k_mixed + saved_x * (1.0 - k_mixed)
    xv = x * v_mixed + saved_x * (1.0 - v_mixed)
    k = mxq(xk, 1, "e4m3") @ mxq(f64(key_weight), 0, "e4m3")
    v = mxq(xv, 1, "e4m3") @ mxq(f64(value_weight), 0, "e4m3")
    w = k + time_first
    p = np.maximum(saved_p, w)
    e1 = np.exp(saved_p - p)
    e2 = np.exp(w - p)
    wkv = (e1 * saved_a + e2 * v) / (e1 * saved_b + e2)
    w2 = saved_p + time_decay
    p2 = np.maximum(w2, k)
    f1 = np.exp(w2 - p2)
    f2 = np.exp(k - p2)
    aa = f1 * saved_a + f2 * v
    bb = f1 * saved_b + f2
    return wkv, aa, bb, p2

@@ -1,0 +1,342 @@
+from contextlib import ExitStack
+
+import concourse.mybir as mybir
+from concourse.masks import make_identity
+
+F32 = mybir.dt.float32
+BF16 = mybir.dt.bfloat16
+U32 = mybir.dt.uint32
+U8 = mybir.dt.uint8
+FP8X4 = mybir.dt.float8_e4m3fn_x4
+ALU = mybir.AluOpType
+ACT = mybir.ActivationFunctionType
+
+P = 128
+B, D, A = 6144, 512, 128
+PACK = 4
+HALVES = 2
+PAIR = 2
+ROWS_PER_PARTITION = B // P
+TILES = 4
+GROUP = TILES * P
+GROUPS = B // GROUP
+LN_BATCH = 4
+
+FLOPS = 2 * 2 * B * D * A
+
+
+def tile_rwkv_attention_pa_t_kernel(
+    tc,
+    x,
+    saved_x,
+    saved_a,
+    saved_b,
+    saved_p,
+    time_decay,
+    time_first,
+    k_mixed,
+    v_mixed,
+    key_weight,
+    value_weight,
+    wkv_out,
+    aa_out,
+    bb_out,
+    p2_out,
+):
+    nc = tc.nc
+
+    def by_partition(dram):
+        return dram.rearrange("(p n) c -> p n c", n=ROWS_PER_PARTITION)
+
+    x_rows, sx_rows = by_partition(x), by_partition(saved_x)
+    sa_rows, sb_rows, sp_rows = by_partition(saved_a), by_partition(saved_b), by_partition(saved_p)
+    wkv_rows, aa_rows = by_partition(wkv_out), by_partition(aa_out)
+    bb_rows, p2_rows = by_partition(bb_out), by_partition(p2_out)
+
+    def rows_of(g):
+        return slice(g * TILES, (g + 1) * TILES)
+
+    def in_range(g):
+        return 0 <= g < GROUPS
+
+    with ExitStack() as stack:
+        const = stack.enter_context(tc.tile_pool(name="const", bufs=1))
+        sbuf = stack.enter_context(tc.tile_pool(name="sbuf", bufs=2))
+        psum = stack.enter_context(tc.psum_pool(name="psum", bufs=1))
+        stack.enter_context(tc.manual_schedule())
+
+        identity = const.tile([P, P], F32, name="identity")
+        make_identity(nc, identity[:])
+
+        mix_rows = const.tile([P, D], BF16, name="mix_rows")
+        nc.vector.memset(mix_rows[:], 0.0)
+        nc.scalar.dma_start(out=mix_rows[0:1, :], in_=k_mixed.unsqueeze(0))
+        nc.scalar.dma_start(out=mix_rows[1:2, :], in_=v_mixed.unsqueeze(0))
+
+        w_raw = const.tile([P, 2, PACK, A], BF16, name="w_raw")
+        for c, weight in enumerate((key_weight, value_weight)):
+            for u in range(HALVES):
+                nc.scalar.dma_start(
+                    out=w_raw[:, c, PAIR * u : PAIR * (u + 1), :],
+                    in_=weight[u * PAIR * P : (u + 1) * PAIR * P, :].rearrange(
+                        "(q e) a -> q e a", e=PAIR
+                    ),
+                )
+        decay_bc = const.tile([P, A], BF16, name="decay_bc")
+        first_bc = const.tile([P, A], BF16, name="first_bc")
+        nc.scalar.dma_start(out=decay_bc[:], in_=time_decay.partition_broadcast(P))
+        nc.scalar.dma_start(out=first_bc[:], in_=time_first.partition_broadcast(P))
+
+        mix_t = psum.tile([P, GROUP], F32, name="mix_t", tag="x_t0")
+        for u in range(HALVES):
+            nc.tensor.transpose(
+                out=mix_t[:, u * P : (u + 1) * P],
+                in_=mix_rows[:].bitcast(F32)[:, u * P : (u + 1) * P],
+                identity=identity[:],
+            )
+        mix = const.tile([P, 2, PACK], F32, name="mix")
+        for u in range(HALVES):
+            first_column = u * P * PAIR
+            nc.vector.tensor_copy(
+                out=mix[:, :, PAIR * u : PAIR * (u + 1)],
+                in_=mix_t[:]
+                .bitcast(BF16)[:, first_column : first_column + 2 * PAIR]
+                .rearrange("q (c e) -> q c e", e=PAIR),
+            )
+        one_minus_mix = const.tile([P, 2, PACK], F32, name="one_minus_mix")
+        nc.vector.tensor_scalar(
+            out=one_minus_mix[:], in0=mix[:], scalar1=-1.0, scalar2=1.0, op0=ALU.mult, op1=ALU.add
+        )
+
+        w_grouped = const.tile([P, 2, A, PACK], BF16, name="w_grouped", align_bytes=64)
+        for c in range(2):
+            nc.vector.tensor_copy(out=w_grouped[:, c], in_=w_raw[:, c].rearrange("q t a -> q a t"))
+        w_codes = const.tile([P, 2 * A], U32, name="w_codes", align_bytes=64)
+        w_scales = const.tile([P, 2 * A], U8, name="w_scales", align_bytes=64)
+        nc.vector.quantize_mx(
+            out=w_codes[:].bitcast(FP8X4),
+            scales=w_scales[:],
+            in_=w_grouped[:].rearrange("q c a t -> q (c a t)"),
+        )
+
+        first_plus_decay = const.tile([P, A], F32, name="first_plus_decay")
+        nc.vector.tensor_tensor(
+            out=first_plus_decay[:], in0=first_bc[:], in1=decay_bc[:], op=ALU.add
+        )
+        two = const.tile([P, 1], F32, name="two")
+        nc.vector.memset(two[:], 2.0)
+
+        def over_tiles(row):
+            return row[:].unsqueeze(1).to_broadcast([P, TILES, A])
+
+        sa_all = const.tile([P, ROWS_PER_PARTITION, A], BF16, name="sa_all")
+        sb_all = const.tile([P, ROWS_PER_PARTITION, A], BF16, name="sb_all")
+        sp_all = const.tile([P, ROWS_PER_PARTITION, A], BF16, name="sp_all")
+
+        live = {}
+
+        def new(name, g, shape, dtype, bufs, pool=sbuf, align_bytes=None):
+            live[name, g] = pool.tile(
+                shape, dtype, name="%s_%d" % (name, g), tag=name, bufs=bufs, align_bytes=align_bytes
+            )
+            return live[name, g]
+
+        def new_f32(name, g, bufs):
+            return new(name, g, [P, TILES, A], F32, bufs)
+
+        def load(g):
+            if not in_range(g):
+                return
+            nc.sync.dma_start(out=new("x", g, [P, TILES, D], BF16, 3)[:], in_=x_rows[:, rows_of(g), :])
+            nc.sync.dma_start(out=new("sx", g, [P, TILES, D], BF16, 3)[:], in_=sx_rows[:, rows_of(g), :])
+            nc.sync.dma_start(out=sp_all[:, rows_of(g), :], in_=sp_rows[:, rows_of(g), :])
+            nc.sync.dma_start(out=sb_all[:, rows_of(g), :], in_=sb_rows[:, rows_of(g), :])
+            nc.sync.dma_start(out=sa_all[:, rows_of(g), :], in_=sa_rows[:, rows_of(g), :])
+
+        def transpose(name, g):
+            if not in_range(g):
+                return
+            words = live[name, g][:].bitcast(F32)
+            for u in range(HALVES):
+                bank = new("%s_t%d" % (name, u), g, [P, GROUP], F32, 1, pool=psum)
+                for j in range(TILES):
+                    nc.tensor.transpose(
+                        out=bank[:, j * P : (j + 1) * P],
+                        in_=words[:, j, u * P : (u + 1) * P],
+                        identity=identity[:],
+                    )
+
+        def value_of_word(name, g, t):
+            u, e = divmod(t, PAIR)
+            bank = live["%s_t%d" % (name, u), g]
+            return bank[:].bitcast(BF16).rearrange("q (r e) -> q e r", e=PAIR)[:, e, :]
+
+        def scale_saved_x(g):
+            if not in_range(g):
+                return
+            for c in range(2):
+                new("scaled%d" % c, g, [P, PACK, GROUP], F32, 2)
+            for t in range(PACK):
+                for c in range(2):
+                    nc.scalar.activation(
+                        out=live["scaled%d" % c, g][:, t, :],
+                        in_=value_of_word("sx", g, t),
+                        func=ACT.Copy,
+                        scale=one_minus_mix[:, c, t : t + 1],
+                    )
+
+        def mix_x(g):
+            if not in_range(g):
+                return
+            for c in range(2):
+                new("mixed%d" % c, g, [P, PACK, GROUP], BF16, 2)
+            for t in range(PACK):
+                for c in range(2):
+                    nc.vector.scalar_tensor_tensor(
+                        out=live["mixed%d" % c, g][:, t, :],
+                        in0=value_of_word("x", g, t),
+                        scalar=mix[:, c, t : t + 1],
+                        in1=live["scaled%d" % c, g][:, t, :],
+                        op0=ALU.mult,
+                        op1=ALU.add,
+                    )
+
+        def group_words(g):
+            if not in_range(g):
+                return
+            for c in range(2):
+                grouped = new("grouped%d" % c, g, [P, GROUP, PACK], BF16, 1, align_bytes=64)
+                nc.scalar.copy(
+                    out=grouped[:].rearrange("q (n i) t -> q n t i", i=4),
+                    in_=live["mixed%d" % c, g][:].rearrange("q t (n i) -> q n t i", i=4),
+                )
+
+        def quantise(g):
+            if not in_range(g):
+                return
+            for c in range(2):
+                codes = new("codes%d" % c, g, [P, GROUP], U32, 2, align_bytes=64)
+                scales = new("scales%d" % c, g, [P, GROUP], U8, 2, align_bytes=64)
+                nc.vector.quantize_mx(
+                    out=codes[:].bitcast(FP8X4),
+                    scales=scales[:],
+                    in_=live["grouped%d" % c, g][:].rearrange("q r t -> q (r t)"),
+                )
+
+        def project(g):
+            if not in_range(g):
+                return
+            for c, (name, bufs) in enumerate((("k", 1), ("v", 2))):
+                bank = new(name, g, [P, TILES, A], F32, bufs, pool=psum)
+                for j in range(TILES):
+                    tile_rows = slice(j * P, (j + 1) * P)
+                    nc.tensor.matmul_mx(
+                        out=bank[:, j, :],
+                        lhsT=live["codes%d" % c, g][:, tile_rows].bitcast(FP8X4),
+                        lhsT_scale=live["scales%d" % c, g][:, tile_rows],
+                        rhs=w_codes[:, c * A : (c + 1) * A].bitcast(FP8X4),
+                        rhs_scale=w_scales[:, c * A : (c + 1) * A],
+                        start=True,
+                        stop=True,
+                    )
+
+        def prepare_state(g):
+            if not in_range(g):
+                return
+            nc.gpsimd.tensor_tensor(
+                out=new_f32("w2", g, 2)[:], in0=sp_all[:, rows_of(g), :], in1=over_tiles(decay_bc), op=ALU.add
+            )
+            nc.gpsimd.tensor_scalar(
+                out=new_f32("one_minus_sb", g, 3)[:],
+                in0=sb_all[:, rows_of(g), :],
+                scalar1=-1.0,
+                scalar2=1.0,
+                op0=ALU.mult,
+                op1=ALU.add,
+            )
+
+        def compare(g):
+            if not in_range(g):
+                return
+            k, v, w2 = live["k", g], live["v", g], live["w2", g]
+            nc.vector.tensor_tensor(out=new_f32("d2", g, 2)[:], in0=k[:], in1=w2[:], op=ALU.subtract)
+            nc.vector.tensor_tensor(out=new_f32("p2", g, 2)[:], in0=k[:], in1=w2[:], op=ALU.max)
+            nc.vector.tensor_tensor(
+                out=new_f32("v_minus_sa", g, 2)[:], in0=v[:], in1=sa_all[:, rows_of(g), :], op=ALU.subtract
+            )
+            nc.sync.dma_start(out=p2_rows[:, rows_of(g), :], in_=live["p2", g][:])
+            nc.gpsimd.tensor_tensor(
+                out=new_f32("d", g, 2)[:], in0=live["d2", g][:], in1=over_tiles(first_plus_decay), op=ALU.add
+            )
+
+        def exponentials(g):
+            if not in_range(g):
+                return
+            d2, d = live["d2", g], live["d", g]
+            nc.scalar.activation(out=new_f32("exp_up", g, 2)[:], in_=d2[:], func=ACT.Exp)
+            nc.scalar.activation(out=new_f32("exp_down", g, 2)[:], in_=d2[:], func=ACT.Exp, scale=-1.0)
+            nc.scalar.activation(out=new_f32("th", g, 2)[:], in_=d[:], func=ACT.Tanh, scale=0.5)
+
+        def blend(g):
+            if not in_range(g):
+                return
+            sa, sb = sa_all[:, rows_of(g), :], sb_all[:, rows_of(g), :]
+            v, th = live["v", g], live["th", g]
+            up, down = live["exp_up", g], live["exp_down", g]
+            stt = nc.vector.scalar_tensor_tensor
+            f1_sa, f2_v, f1_sb = new_f32("f1_sa", g, 1), new_f32("f2_v", g, 1), new_f32("f1_sb", g, 1)
+            aa, bb = new_f32("aa", g, 2), new_f32("bb", g, 2)
+            stt(out=f2_v[:], in0=up[:], scalar=1.0, in1=v[:], op0=ALU.min, op1=ALU.mult)
+            stt(out=f1_sa[:], in0=down[:], scalar=1.0, in1=sa, op0=ALU.min, op1=ALU.mult)
+            nc.vector.tensor_tensor(out=aa[:], in0=f1_sa[:], in1=f2_v[:], op=ALU.add)
+            nc.sync.dma_start(out=aa_rows[:, rows_of(g), :], in_=aa[:])
+            stt(out=f1_sb[:], in0=down[:], scalar=1.0, in1=sb, op0=ALU.min, op1=ALU.mult)
+            stt(out=bb[:], in0=up[:], scalar=1.0, in1=f1_sb[:], op0=ALU.min, op1=ALU.add)
+            nc.sync.dma_start(out=bb_rows[:, rows_of(g), :], in_=bb[:])
+            pull, num = new_f32("pull", g, 1), new_f32("num", g, 1)
+            stt(out=pull[:], in0=th[:], scalar=1.0, in1=live["v_minus_sa", g][:], op0=ALU.subtract, op1=ALU.mult)
+            stt(out=num[:], in0=v[:], scalar=2.0, in1=pull[:], op0=ALU.mult, op1=ALU.add)
+            den_minus_2 = new_f32("den_minus_2", g, 2)
+            stt(out=den_minus_2[:], in0=th[:], scalar=1.0, in1=live["one_minus_sb", g][:], op0=ALU.subtract, op1=ALU.mult)
+            stt(out=new_f32("num_den", g, LN_BATCH + 1)[:], in0=den_minus_2[:], scalar=2.0, in1=num[:], op0=ALU.add, op1=ALU.mult)
+
+        def square_den(g):
+            if not in_range(g):
+                return
+            nc.scalar.activation(
+                out=new_f32("inv_den2", g, LN_BATCH)[:], in_=live["den_minus_2", g][:], func=ACT.Square, bias=two[:, 0:1]
+            )
+
+        def batch_ending_at(g):
+            if in_range(g) and (g + 1) % LN_BATCH == 0:
+                return range(g + 1 - LN_BATCH, g + 1)
+            return range(0)
+
+        def invert_den2(last):
+            for g in batch_ending_at(last):
+                nc.scalar.activation(out=live["inv_den2", g][:], in_=live["inv_den2", g][:], func=ACT.Ln)
+            for g in batch_ending_at(last):
+                nc.scalar.activation(out=live["inv_den2", g][:], in_=live["inv_den2", g][:], func=ACT.Exp, scale=-1.0)
+
+        def divide(last):
+            for g in batch_ending_at(last):
+                wkv = new_f32("wkv", g, LN_BATCH)
+                nc.vector.tensor_tensor(out=wkv[:], in0=live["num_den", g][:], in1=live["inv_den2", g][:], op=ALU.mult)
+                nc.sync.dma_start(out=wkv_rows[:, rows_of(g), :], in_=wkv[:])
+
+        for i in range(-2, GROUPS + 4):
+            load(i + 2)
+            scale_saved_x(i)
+            transpose("sx", i + 1)
+            blend(i - 3)
+            compare(i - 2)
+            divide(i - 4)
+            mix_x(i)
+            transpose("x", i + 1)
+            group_words(i - 1)
+            quantise(i - 1)
+            project(i - 1)
+            exponentials(i - 2)
+            prepare_state(i - 1)
+            square_den(i - 3)
+            invert_den2(i - 3)

@@ -20,7 +20,8 @@ ROWS_PER_PARTITION = B // P
 TILES = 4
 GROUP = TILES * P
 GROUPS = B // GROUP
-LN_BATCH = 4
+VECTOR_TILES = 1
+LN_BATCH = 5
 
 FLOPS = 2 * 2 * B * D * A
 
@@ -147,8 +148,8 @@ def tile_rwkv_attention_pa_t_kernel(
         def load(g):
             if not in_range(g):
                 return
-            nc.sync.dma_start(out=new("x", g, [P, TILES, D], BF16, 3)[:], in_=x_rows[:, rows_of(g), :])
             nc.sync.dma_start(out=new("sx", g, [P, TILES, D], BF16, 3)[:], in_=sx_rows[:, rows_of(g), :])
+            nc.sync.dma_start(out=new("x", g, [P, TILES, D], BF16, 3)[:], in_=x_rows[:, rows_of(g), :])
             nc.sync.dma_start(out=sp_all[:, rows_of(g), :], in_=sp_rows[:, rows_of(g), :])
             nc.sync.dma_start(out=sb_all[:, rows_of(g), :], in_=sb_rows[:, rows_of(g), :])
             nc.sync.dma_start(out=sa_all[:, rows_of(g), :], in_=sa_rows[:, rows_of(g), :])
@@ -201,14 +202,16 @@ def tile_rwkv_attention_pa_t_kernel(
                         op1=ALU.add,
                     )
 
-        def group_words(g):
+        def group_words(g, engine_copy, first_tile, last_tile):
             if not in_range(g):
                 return
+            rows = slice(first_tile * P, last_tile * P)
             for c in range(2):
-                grouped = new("grouped%d" % c, g, [P, GROUP, PACK], BF16, 1, align_bytes=64)
-                nc.scalar.copy(
-                    out=grouped[:].rearrange("q (n i) t -> q n t i", i=4),
-                    in_=live["mixed%d" % c, g][:].rearrange("q t (n i) -> q n t i", i=4),
+                if ("grouped%d" % c, g) not in live:
+                    new("grouped%d" % c, g, [P, GROUP, PACK], BF16, 1, align_bytes=64)
+                engine_copy(
+                    out=live["grouped%d" % c, g][:, rows, :].rearrange("q (n i) t -> q n t i", i=4),
+                    in_=live["mixed%d" % c, g][:, :, rows].rearrange("q t (n i) -> q n t i", i=4),
                 )
 
         def quantise(g):
@@ -277,28 +280,33 @@ def tile_rwkv_attention_pa_t_kernel(
             nc.scalar.activation(out=new_f32("exp_down", g, 2)[:], in_=d2[:], func=ACT.Exp, scale=-1.0)
             nc.scalar.activation(out=new_f32("th", g, 2)[:], in_=d[:], func=ACT.Tanh, scale=0.5)
 
-        def blend(g):
+        def weigh_wkv(g):
+            if not in_range(g):
+                return
+            v, th = live["v", g], live["th", g]
+            stt = nc.vector.scalar_tensor_tensor
+            pull, num = new_f32("pull", g, 1), new_f32("num", g, 1)
+            den_minus_2 = new_f32("den_minus_2", g, 2)
+            stt(out=den_minus_2[:], in0=th[:], scalar=1.0, in1=live["one_minus_sb", g][:], op0=ALU.subtract, op1=ALU.mult)
+            stt(out=pull[:], in0=th[:], scalar=1.0, in1=live["v_minus_sa", g][:], op0=ALU.subtract, op1=ALU.mult)
+            stt(out=num[:], in0=v[:], scalar=2.0, in1=pull[:], op0=ALU.mult, op1=ALU.add)
+            stt(out=new_f32("num_den", g, LN_BATCH + 1)[:], in0=den_minus_2[:], scalar=2.0, in1=num[:], op0=ALU.add, op1=ALU.mult)
+
+        def update_state(g):
             if not in_range(g):
                 return
             sa, sb = sa_all[:, rows_of(g), :], sb_all[:, rows_of(g), :]
-            v, th = live["v", g], live["th", g]
-            up, down = live["exp_up", g], live["exp_down", g]
+            v, up, down = live["v", g], live["exp_up", g], live["exp_down", g]
             stt = nc.vector.scalar_tensor_tensor
-            f1_sa, f2_v, f1_sb = new_f32("f1_sa", g, 1), new_f32("f2_v", g, 1), new_f32("f1_sb", g, 1)
+            f1_sa, f2_v, f1_sb = new_f32("f1_sa", g, 2), new_f32("f2_v", g, 2), new_f32("f1_sb", g, 1)
             aa, bb = new_f32("aa", g, 2), new_f32("bb", g, 2)
             stt(out=f2_v[:], in0=up[:], scalar=1.0, in1=v[:], op0=ALU.min, op1=ALU.mult)
             stt(out=f1_sa[:], in0=down[:], scalar=1.0, in1=sa, op0=ALU.min, op1=ALU.mult)
-            nc.vector.tensor_tensor(out=aa[:], in0=f1_sa[:], in1=f2_v[:], op=ALU.add)
+            nc.gpsimd.tensor_tensor(out=aa[:], in0=f1_sa[:], in1=f2_v[:], op=ALU.add)
             nc.sync.dma_start(out=aa_rows[:, rows_of(g), :], in_=aa[:])
             stt(out=f1_sb[:], in0=down[:], scalar=1.0, in1=sb, op0=ALU.min, op1=ALU.mult)
             stt(out=bb[:], in0=up[:], scalar=1.0, in1=f1_sb[:], op0=ALU.min, op1=ALU.add)
             nc.sync.dma_start(out=bb_rows[:, rows_of(g), :], in_=bb[:])
-            pull, num = new_f32("pull", g, 1), new_f32("num", g, 1)
-            stt(out=pull[:], in0=th[:], scalar=1.0, in1=live["v_minus_sa", g][:], op0=ALU.subtract, op1=ALU.mult)
-            stt(out=num[:], in0=v[:], scalar=2.0, in1=pull[:], op0=ALU.mult, op1=ALU.add)
-            den_minus_2 = new_f32("den_minus_2", g, 2)
-            stt(out=den_minus_2[:], in0=th[:], scalar=1.0, in1=live["one_minus_sb", g][:], op0=ALU.subtract, op1=ALU.mult)
-            stt(out=new_f32("num_den", g, LN_BATCH + 1)[:], in0=den_minus_2[:], scalar=2.0, in1=num[:], op0=ALU.add, op1=ALU.mult)
 
         def square_den(g):
             if not in_range(g):
@@ -308,8 +316,8 @@ def tile_rwkv_attention_pa_t_kernel(
             )
 
         def batch_ending_at(g):
-            if in_range(g) and (g + 1) % LN_BATCH == 0:
-                return range(g + 1 - LN_BATCH, g + 1)
+            if in_range(g) and ((g + 1) % LN_BATCH == 0 or g == GROUPS - 1):
+                return range(g // LN_BATCH * LN_BATCH, g + 1)
             return range(0)
 
         def invert_den2(last):
@@ -320,23 +328,25 @@ def tile_rwkv_attention_pa_t_kernel(
 
         def divide(last):
             for g in batch_ending_at(last):
-                wkv = new_f32("wkv", g, LN_BATCH)
-                nc.vector.tensor_tensor(out=wkv[:], in0=live["num_den", g][:], in1=live["inv_den2", g][:], op=ALU.mult)
+                wkv = new_f32("wkv", g, 3)
+                nc.gpsimd.tensor_tensor(out=wkv[:], in0=live["num_den", g][:], in1=live["inv_den2", g][:], op=ALU.mult)
                 nc.sync.dma_start(out=wkv_rows[:, rows_of(g), :], in_=wkv[:])
 
         for i in range(-2, GROUPS + 4):
             load(i + 2)
             scale_saved_x(i)
             transpose("sx", i + 1)
-            blend(i - 3)
+            group_words(i - 1, nc.vector.tensor_copy, 0, VECTOR_TILES)
+            weigh_wkv(i - 3)
+            update_state(i - 3)
             compare(i - 2)
             divide(i - 4)
+            prepare_state(i - 1)
             mix_x(i)
             transpose("x", i + 1)
-            group_words(i - 1)
+            group_words(i - 1, nc.scalar.copy, VECTOR_TILES, TILES)
             quantise(i - 1)
             project(i - 1)
-            exponentials(i - 2)
-            prepare_state(i - 1)
             square_den(i - 3)
+            exponentials(i - 2)
             invert_den2(i - 3)

@@ -280,32 +280,26 @@ def tile_rwkv_attention_pa_t_kernel(
             nc.scalar.activation(out=new_f32("exp_down", g, 2)[:], in_=d2[:], func=ACT.Exp, scale=-1.0)
             nc.scalar.activation(out=new_f32("th", g, 2)[:], in_=d[:], func=ACT.Tanh, scale=0.5)
 
-        def weigh_wkv(g):
-            if not in_range(g):
-                return
-            v, th = live["v", g], live["th", g]
-            stt = nc.vector.scalar_tensor_tensor
-            pull, num = new_f32("pull", g, 1), new_f32("num", g, 1)
-            den_minus_2 = new_f32("den_minus_2", g, 2)
-            stt(out=den_minus_2[:], in0=th[:], scalar=1.0, in1=live["one_minus_sb", g][:], op0=ALU.subtract, op1=ALU.mult)
-            stt(out=pull[:], in0=th[:], scalar=1.0, in1=live["v_minus_sa", g][:], op0=ALU.subtract, op1=ALU.mult)
-            stt(out=num[:], in0=v[:], scalar=2.0, in1=pull[:], op0=ALU.mult, op1=ALU.add)
-            stt(out=new_f32("num_den", g, LN_BATCH + 1)[:], in0=den_minus_2[:], scalar=2.0, in1=num[:], op0=ALU.add, op1=ALU.mult)
-
-        def update_state(g):
+        def blend(g):
             if not in_range(g):
                 return
             sa, sb = sa_all[:, rows_of(g), :], sb_all[:, rows_of(g), :]
-            v, up, down = live["v", g], live["exp_up", g], live["exp_down", g]
+            v, th, up, down = live["v", g], live["th", g], live["exp_up", g], live["exp_down", g]
             stt = nc.vector.scalar_tensor_tensor
-            f1_sa, f2_v, f1_sb = new_f32("f1_sa", g, 2), new_f32("f2_v", g, 2), new_f32("f1_sb", g, 1)
+            pull, num, f1_sb = new_f32("pull", g, 1), new_f32("num", g, 1), new_f32("f1_sb", g, 1)
+            f1_sa, f2_v = new_f32("f1_sa", g, 2), new_f32("f2_v", g, 2)
+            den_minus_2, num_den = new_f32("den_minus_2", g, 2), new_f32("num_den", g, LN_BATCH + 1)
             aa, bb = new_f32("aa", g, 2), new_f32("bb", g, 2)
+            stt(out=den_minus_2[:], in0=th[:], scalar=1.0, in1=live["one_minus_sb", g][:], op0=ALU.subtract, op1=ALU.mult)
+            stt(out=pull[:], in0=th[:], scalar=1.0, in1=live["v_minus_sa", g][:], op0=ALU.subtract, op1=ALU.mult)
             stt(out=f2_v[:], in0=up[:], scalar=1.0, in1=v[:], op0=ALU.min, op1=ALU.mult)
+            stt(out=num[:], in0=v[:], scalar=2.0, in1=pull[:], op0=ALU.mult, op1=ALU.add)
             stt(out=f1_sa[:], in0=down[:], scalar=1.0, in1=sa, op0=ALU.min, op1=ALU.mult)
+            stt(out=f1_sb[:], in0=down[:], scalar=1.0, in1=sb, op0=ALU.min, op1=ALU.mult)
+            stt(out=num_den[:], in0=den_minus_2[:], scalar=2.0, in1=num[:], op0=ALU.add, op1=ALU.mult)
+            stt(out=bb[:], in0=up[:], scalar=1.0, in1=f1_sb[:], op0=ALU.min, op1=ALU.add)
             nc.gpsimd.tensor_tensor(out=aa[:], in0=f1_sa[:], in1=f2_v[:], op=ALU.add)
             nc.sync.dma_start(out=aa_rows[:, rows_of(g), :], in_=aa[:])
-            stt(out=f1_sb[:], in0=down[:], scalar=1.0, in1=sb, op0=ALU.min, op1=ALU.mult)
-            stt(out=bb[:], in0=up[:], scalar=1.0, in1=f1_sb[:], op0=ALU.min, op1=ALU.add)
             nc.sync.dma_start(out=bb_rows[:, rows_of(g), :], in_=bb[:])
 
         def square_den(g):
@@ -337,8 +331,7 @@ def tile_rwkv_attention_pa_t_kernel(
             scale_saved_x(i)
             transpose("sx", i + 1)
             group_words(i - 1, nc.vector.tensor_copy, 0, VECTOR_TILES)
-            weigh_wkv(i - 3)
-            update_state(i - 3)
+            blend(i - 3)
             compare(i - 2)
             divide(i - 4)
             prepare_state(i - 1)

@@ -323,7 +323,7 @@ def tile_rwkv_attention_pa_t_kernel(
         def divide(last):
             for g in batch_ending_at(last):
                 wkv = new_f32("wkv", g, 3)
-                nc.gpsimd.tensor_tensor(out=wkv[:], in0=live["num_den", g][:], in1=live["inv_den2", g][:], op=ALU.mult)
+                nc.vector.tensor_tensor(out=wkv[:], in0=live["num_den", g][:], in1=live["inv_den2", g][:], op=ALU.mult)
                 nc.sync.dma_start(out=wkv_rows[:, rows_of(g), :], in_=wkv[:])
 
         for i in range(-2, GROUPS + 4):
@@ -332,8 +332,8 @@ def tile_rwkv_attention_pa_t_kernel(
             transpose("sx", i + 1)
             group_words(i - 1, nc.vector.tensor_copy, 0, VECTOR_TILES)
             blend(i - 3)
-            compare(i - 2)
             divide(i - 4)
+            compare(i - 2)
             prepare_state(i - 1)
             mix_x(i)
             transpose("x", i + 1)

@@ -22,6 +22,8 @@ GROUP = TILES * P
 GROUPS = B // GROUP
 VECTOR_TILES = 1
 LN_BATCH = 5
+BLEND_LAG = 3
+DIVIDE_LAG = BLEND_LAG + LN_BATCH
 
 FLOPS = 2 * 2 * B * D * A
 
@@ -130,8 +132,10 @@ def tile_rwkv_attention_pa_t_kernel(
         def over_tiles(row):
             return row[:].unsqueeze(1).to_broadcast([P, TILES, A])
 
-        sa_all = const.tile([P, ROWS_PER_PARTITION, A], BF16, name="sa_all")
-        sb_all = const.tile([P, ROWS_PER_PARTITION, A], BF16, name="sb_all")
+        def twice(tile):
+            return tile[:].unsqueeze(1).to_broadcast([P, 2, TILES, A])
+
+        sab_all = const.tile([P, GROUPS, 2, TILES, A], BF16, name="sab_all")
         sp_all = const.tile([P, ROWS_PER_PARTITION, A], BF16, name="sp_all")
 
         live = {}
@@ -145,14 +149,17 @@ def tile_rwkv_attention_pa_t_kernel(
         def new_f32(name, g, bufs):
             return new(name, g, [P, TILES, A], F32, bufs)
 
+        def new_f32_pair(name, g, bufs):
+            return new(name, g, [P, 2, TILES, A], F32, bufs)
+
         def load(g):
             if not in_range(g):
                 return
-            nc.sync.dma_start(out=new("sx", g, [P, TILES, D], BF16, 3)[:], in_=sx_rows[:, rows_of(g), :])
-            nc.sync.dma_start(out=new("x", g, [P, TILES, D], BF16, 3)[:], in_=x_rows[:, rows_of(g), :])
+            nc.sync.dma_start(out=new("sx", g, [P, TILES, D], BF16, 2)[:], in_=sx_rows[:, rows_of(g), :])
+            nc.sync.dma_start(out=new("x", g, [P, TILES, D], BF16, 2)[:], in_=x_rows[:, rows_of(g), :])
             nc.sync.dma_start(out=sp_all[:, rows_of(g), :], in_=sp_rows[:, rows_of(g), :])
-            nc.sync.dma_start(out=sb_all[:, rows_of(g), :], in_=sb_rows[:, rows_of(g), :])
-            nc.sync.dma_start(out=sa_all[:, rows_of(g), :], in_=sa_rows[:, rows_of(g), :])
+            nc.sync.dma_start(out=sab_all[:, g, 1], in_=sb_rows[:, rows_of(g), :])
+            nc.sync.dma_start(out=sab_all[:, g, 0], in_=sa_rows[:, rows_of(g), :])
 
         def transpose(name, g):
             if not in_range(g):
@@ -175,12 +182,11 @@ def tile_rwkv_attention_pa_t_kernel(
         def scale_saved_x(g):
             if not in_range(g):
                 return
-            for c in range(2):
-                new("scaled%d" % c, g, [P, PACK, GROUP], F32, 2)
+            scaled = new("scaled", g, [P, 2, PACK, GROUP], F32, 2)
             for t in range(PACK):
                 for c in range(2):
                     nc.scalar.activation(
-                        out=live["scaled%d" % c, g][:, t, :],
+                        out=scaled[:, c, t, :],
                         in_=value_of_word("sx", g, t),
                         func=ACT.Copy,
                         scale=one_minus_mix[:, c, t : t + 1],
@@ -189,54 +195,56 @@ def tile_rwkv_attention_pa_t_kernel(
         def mix_x(g):
             if not in_range(g):
                 return
-            for c in range(2):
-                new("mixed%d" % c, g, [P, PACK, GROUP], BF16, 2)
+            mixed = new("mixed", g, [P, 2, PACK, GROUP], BF16, 2)
             for t in range(PACK):
                 for c in range(2):
                     nc.vector.scalar_tensor_tensor(
-                        out=live["mixed%d" % c, g][:, t, :],
+                        out=mixed[:, c, t, :],
                         in0=value_of_word("x", g, t),
                         scalar=mix[:, c, t : t + 1],
-                        in1=live["scaled%d" % c, g][:, t, :],
+                        in1=live["scaled", g][:, c, t, :],
                         op0=ALU.mult,
                         op1=ALU.add,
                     )
 
-        def group_words(g, engine_copy, first_tile, last_tile):
+        def group_words(g):
             if not in_range(g):
                 return
-            rows = slice(first_tile * P, last_tile * P)
+            mixed = live["mixed", g]
+            grouped = new("grouped", g, [P, 2, GROUP, PACK], BF16, 1, align_bytes=64)
+            split = VECTOR_TILES * P
+            nc.vector.tensor_copy(
+                out=grouped[:, :, :split, :].rearrange("q c (n i) t -> q c n t i", i=4),
+                in_=mixed[:, :, :, :split].rearrange("q c t (n i) -> q c n t i", i=4),
+            )
             for c in range(2):
-                if ("grouped%d" % c, g) not in live:
-                    new("grouped%d" % c, g, [P, GROUP, PACK], BF16, 1, align_bytes=64)
-                engine_copy(
-                    out=live["grouped%d" % c, g][:, rows, :].rearrange("q (n i) t -> q n t i", i=4),
-                    in_=live["mixed%d" % c, g][:, :, rows].rearrange("q t (n i) -> q n t i", i=4),
+                nc.scalar.copy(
+                    out=grouped[:, c, split:, :].rearrange("q (n i) t -> q n t i", i=4),
+                    in_=mixed[:, c, :, split:].rearrange("q t (n i) -> q n t i", i=4),
                 )
 
         def quantise(g):
             if not in_range(g):
                 return
-            for c in range(2):
-                codes = new("codes%d" % c, g, [P, GROUP], U32, 2, align_bytes=64)
-                scales = new("scales%d" % c, g, [P, GROUP], U8, 2, align_bytes=64)
-                nc.vector.quantize_mx(
-                    out=codes[:].bitcast(FP8X4),
-                    scales=scales[:],
-                    in_=live["grouped%d" % c, g][:].rearrange("q r t -> q (r t)"),
-                )
+            codes = new("codes", g, [P, 2, GROUP], U32, 2, align_bytes=64)
+            scales = new("scales", g, [P, 2, GROUP], U8, 2, align_bytes=64)
+            nc.vector.quantize_mx(
+                out=codes[:].rearrange("q c r -> q (c r)").bitcast(FP8X4),
+                scales=scales[:].rearrange("q c r -> q (c r)"),
+                in_=live["grouped", g][:].rearrange("q c r t -> q (c r t)"),
+            )
 
         def project(g):
             if not in_range(g):
                 return
-            for c, (name, bufs) in enumerate((("k", 1), ("v", 2))):
+            for c, (name, bufs) in enumerate((("k", 1), ("v", 3))):
                 bank = new(name, g, [P, TILES, A], F32, bufs, pool=psum)
                 for j in range(TILES):
                     tile_rows = slice(j * P, (j + 1) * P)
                     nc.tensor.matmul_mx(
                         out=bank[:, j, :],
-                        lhsT=live["codes%d" % c, g][:, tile_rows].bitcast(FP8X4),
-                        lhsT_scale=live["scales%d" % c, g][:, tile_rows],
+                        lhsT=live["codes", g][:, c, tile_rows].bitcast(FP8X4),
+                        lhsT_scale=live["scales", g][:, c, tile_rows],
                         rhs=w_codes[:, c * A : (c + 1) * A].bitcast(FP8X4),
                         rhs_scale=w_scales[:, c * A : (c + 1) * A],
                         start=True,
@@ -250,8 +258,8 @@ def tile_rwkv_attention_pa_t_kernel(
                 out=new_f32("w2", g, 2)[:], in0=sp_all[:, rows_of(g), :], in1=over_tiles(decay_bc), op=ALU.add
             )
             nc.gpsimd.tensor_scalar(
-                out=new_f32("one_minus_sb", g, 3)[:],
-                in0=sb_all[:, rows_of(g), :],
+                out=new_f32_pair("factors", g, 3)[:, 0],
+                in0=sab_all[:, g, 1],
                 scalar1=-1.0,
                 scalar2=1.0,
                 op0=ALU.mult,
@@ -264,9 +272,7 @@ def tile_rwkv_attention_pa_t_kernel(
             k, v, w2 = live["k", g], live["v", g], live["w2", g]
             nc.vector.tensor_tensor(out=new_f32("d2", g, 2)[:], in0=k[:], in1=w2[:], op=ALU.subtract)
             nc.vector.tensor_tensor(out=new_f32("p2", g, 2)[:], in0=k[:], in1=w2[:], op=ALU.max)
-            nc.vector.tensor_tensor(
-                out=new_f32("v_minus_sa", g, 2)[:], in0=v[:], in1=sa_all[:, rows_of(g), :], op=ALU.subtract
-            )
+            nc.vector.tensor_tensor(out=live["factors", g][:, 1], in0=v[:], in1=sab_all[:, g, 0], op=ALU.subtract)
             nc.sync.dma_start(out=p2_rows[:, rows_of(g), :], in_=live["p2", g][:])
             nc.gpsimd.tensor_tensor(
                 out=new_f32("d", g, 2)[:], in0=live["d2", g][:], in1=over_tiles(first_plus_decay), op=ALU.add
@@ -283,22 +289,19 @@ def tile_rwkv_attention_pa_t_kernel(
         def blend(g):
             if not in_range(g):
                 return
-            sa, sb = sa_all[:, rows_of(g), :], sb_all[:, rows_of(g), :]
             v, th, up, down = live["v", g], live["th", g], live["exp_up", g], live["exp_down", g]
             stt = nc.vector.scalar_tensor_tensor
-            pull, num, f1_sb = new_f32("pull", g, 1), new_f32("num", g, 1), new_f32("f1_sb", g, 1)
-            f1_sa, f2_v = new_f32("f1_sa", g, 2), new_f32("f2_v", g, 2)
-            den_minus_2, num_den = new_f32("den_minus_2", g, 2), new_f32("num_den", g, LN_BATCH + 1)
+            pulls = new_f32_pair("pulls", g, 2)
+            f1_state = new_f32_pair("f1_state", g, 2)
+            f2_v, num = new_f32("f2_v", g, 2), new_f32("num", g, 1)
             aa, bb = new_f32("aa", g, 2), new_f32("bb", g, 2)
-            stt(out=den_minus_2[:], in0=th[:], scalar=1.0, in1=live["one_minus_sb", g][:], op0=ALU.subtract, op1=ALU.mult)
-            stt(out=pull[:], in0=th[:], scalar=1.0, in1=live["v_minus_sa", g][:], op0=ALU.subtract, op1=ALU.mult)
+            stt(out=pulls[:], in0=twice(th), scalar=1.0, in1=live["factors", g][:], op0=ALU.subtract, op1=ALU.mult)
             stt(out=f2_v[:], in0=up[:], scalar=1.0, in1=v[:], op0=ALU.min, op1=ALU.mult)
-            stt(out=num[:], in0=v[:], scalar=2.0, in1=pull[:], op0=ALU.mult, op1=ALU.add)
-            stt(out=f1_sa[:], in0=down[:], scalar=1.0, in1=sa, op0=ALU.min, op1=ALU.mult)
-            stt(out=f1_sb[:], in0=down[:], scalar=1.0, in1=sb, op0=ALU.min, op1=ALU.mult)
-            stt(out=num_den[:], in0=den_minus_2[:], scalar=2.0, in1=num[:], op0=ALU.add, op1=ALU.mult)
-            stt(out=bb[:], in0=up[:], scalar=1.0, in1=f1_sb[:], op0=ALU.min, op1=ALU.add)
-            nc.gpsimd.tensor_tensor(out=aa[:], in0=f1_sa[:], in1=f2_v[:], op=ALU.add)
+            stt(out=f1_state[:], in0=twice(down), scalar=1.0, in1=sab_all[:, g], op0=ALU.min, op1=ALU.mult)
+            stt(out=num[:], in0=v[:], scalar=2.0, in1=pulls[:, 1], op0=ALU.mult, op1=ALU.add)
+            stt(out=bb[:], in0=up[:], scalar=1.0, in1=f1_state[:, 1], op0=ALU.min, op1=ALU.add)
+            stt(out=new_f32("num_den", g, LN_BATCH + 1)[:], in0=pulls[:, 0], scalar=2.0, in1=num[:], op0=ALU.add, op1=ALU.mult)
+            nc.gpsimd.tensor_tensor(out=aa[:], in0=f1_state[:, 0], in1=f2_v[:], op=ALU.add)
             nc.sync.dma_start(out=aa_rows[:, rows_of(g), :], in_=aa[:])
             nc.sync.dma_start(out=bb_rows[:, rows_of(g), :], in_=bb[:])
 
@@ -306,40 +309,51 @@ def tile_rwkv_attention_pa_t_kernel(
             if not in_range(g):
                 return
             nc.scalar.activation(
-                out=new_f32("inv_den2", g, LN_BATCH)[:], in_=live["den_minus_2", g][:], func=ACT.Square, bias=two[:, 0:1]
+                out=new_f32("inv_den2", g, LN_BATCH)[:], in_=live["pulls", g][:, 0], func=ACT.Square, bias=two[:, 0:1]
             )
 
-        def batch_ending_at(g):
-            if in_range(g) and ((g + 1) % LN_BATCH == 0 or g == GROUPS - 1):
-                return range(g // LN_BATCH * LN_BATCH, g + 1)
-            return range(0)
-
         def invert_den2(last):
-            for g in batch_ending_at(last):
+            if not (in_range(last) and ((last + 1) % LN_BATCH == 0 or last == GROUPS - 1)):
+                return
+            batch = range(last // LN_BATCH * LN_BATCH, last + 1)
+            for g in batch:
                 nc.scalar.activation(out=live["inv_den2", g][:], in_=live["inv_den2", g][:], func=ACT.Ln)
-            for g in batch_ending_at(last):
+            for g in batch:
                 nc.scalar.activation(out=live["inv_den2", g][:], in_=live["inv_den2", g][:], func=ACT.Exp, scale=-1.0)
 
-        def divide(last):
-            for g in batch_ending_at(last):
-                wkv = new_f32("wkv", g, 3)
-                nc.vector.tensor_tensor(out=wkv[:], in0=live["num_den", g][:], in1=live["inv_den2", g][:], op=ALU.mult)
-                nc.sync.dma_start(out=wkv_rows[:, rows_of(g), :], in_=wkv[:])
+        def divide(g, engine):
+            if not in_range(g):
+                return
+            wkv = new_f32("wkv", g, LN_BATCH)
+            engine.tensor_tensor(out=wkv[:], in0=live["num_den", g][:], in1=live["inv_den2", g][:], op=ALU.mult)
+            nc.sync.dma_start(out=wkv_rows[:, rows_of(g), :], in_=wkv[:])
 
-        for i in range(-2, GROUPS + 4):
+        for i in range(-2, GROUPS):
             load(i + 2)
             scale_saved_x(i)
             transpose("sx", i + 1)
-            group_words(i - 1, nc.vector.tensor_copy, 0, VECTOR_TILES)
-            blend(i - 3)
-            divide(i - 4)
+            group_words(i - 1)
+            blend(i - BLEND_LAG)
             compare(i - 2)
+            divide(i - DIVIDE_LAG, nc.gpsimd)
             prepare_state(i - 1)
             mix_x(i)
             transpose("x", i + 1)
-            group_words(i - 1, nc.scalar.copy, VECTOR_TILES, TILES)
             quantise(i - 1)
             project(i - 1)
-            square_den(i - 3)
+            square_den(i - BLEND_LAG)
             exponentials(i - 2)
-            invert_den2(i - 3)
+            invert_den2(i - BLEND_LAG)
+        for i in range(GROUPS, GROUPS + BLEND_LAG):
+            group_words(i - 1)
+            prepare_state(i - 1)
+            compare(i - 2)
+            divide(i - DIVIDE_LAG, nc.gpsimd)
+            quantise(i - 1)
+            project(i - 1)
+            blend(i - BLEND_LAG)
+            exponentials(i - 2)
+            square_den(i - BLEND_LAG)
+            invert_den2(i - BLEND_LAG)
+        for g in range(GROUPS + BLEND_LAG - DIVIDE_LAG, GROUPS):
+            divide(g, nc.vector)

from contextlib import ExitStack

import concourse.mybir as mybir
from concourse.masks import make_identity

F32 = mybir.dt.float32
BF16 = mybir.dt.bfloat16
U32 = mybir.dt.uint32
U8 = mybir.dt.uint8
FP8X4 = mybir.dt.float8_e4m3fn_x4
ALU = mybir.AluOpType
ACT = mybir.ActivationFunctionType

P = 128
B, D, A = 6144, 512, 128
PACK = 4
HALVES = 2
PAIR = 2
ROWS_PER_PARTITION = B // P
TILES = 4
GROUP = TILES * P
GROUPS = B // GROUP
VECTOR_TILES = 1
LN_BATCH = 5
BLEND_LAG = 3
DIVIDE_LAG = BLEND_LAG + LN_BATCH

FLOPS = 2 * 2 * B * D * A


def tile_rwkv_attention_pa_t_kernel(
    tc,
    x,
    saved_x,
    saved_a,
    saved_b,
    saved_p,
    time_decay,
    time_first,
    k_mixed,
    v_mixed,
    key_weight,
    value_weight,
    wkv_out,
    aa_out,
    bb_out,
    p2_out,
):
    nc = tc.nc

    def by_partition(dram):
        return dram.rearrange("(p n) c -> p n c", n=ROWS_PER_PARTITION)

    x_rows, sx_rows = by_partition(x), by_partition(saved_x)
    sa_rows, sb_rows, sp_rows = by_partition(saved_a), by_partition(saved_b), by_partition(saved_p)
    wkv_rows, aa_rows = by_partition(wkv_out), by_partition(aa_out)
    bb_rows, p2_rows = by_partition(bb_out), by_partition(p2_out)

    def rows_of(g):
        return slice(g * TILES, (g + 1) * TILES)

    def in_range(g):
        return 0 <= g < GROUPS

    with ExitStack() as stack:
        const = stack.enter_context(tc.tile_pool(name="const", bufs=1))
        sbuf = stack.enter_context(tc.tile_pool(name="sbuf", bufs=2))
        psum = stack.enter_context(tc.psum_pool(name="psum", bufs=1))
        stack.enter_context(tc.manual_schedule())

        identity = const.tile([P, P], F32, name="identity")
        make_identity(nc, identity[:])

        mix_rows = const.tile([P, D], BF16, name="mix_rows")
        nc.vector.memset(mix_rows[:], 0.0)
        nc.scalar.dma_start(out=mix_rows[0:1, :], in_=k_mixed.unsqueeze(0))
        nc.scalar.dma_start(out=mix_rows[1:2, :], in_=v_mixed.unsqueeze(0))

        w_raw = const.tile([P, 2, PACK, A], BF16, name="w_raw")
        for c, weight in enumerate((key_weight, value_weight)):
            for u in range(HALVES):
                nc.scalar.dma_start(
                    out=w_raw[:, c, PAIR * u : PAIR * (u + 1), :],
                    in_=weight[u * PAIR * P : (u + 1) * PAIR * P, :].rearrange(
                        "(q e) a -> q e a", e=PAIR
                    ),
                )
        decay_bc = const.tile([P, A], BF16, name="decay_bc")
        first_bc = const.tile([P, A], BF16, name="first_bc")
        nc.scalar.dma_start(out=decay_bc[:], in_=time_decay.partition_broadcast(P))
        nc.scalar.dma_start(out=first_bc[:], in_=time_first.partition_broadcast(P))

        mix_t = psum.tile([P, GROUP], F32, name="mix_t", tag="x_t0")
        for u in range(HALVES):
            nc.tensor.transpose(
                out=mix_t[:, u * P : (u + 1) * P],
                in_=mix_rows[:].bitcast(F32)[:, u * P : (u + 1) * P],
                identity=identity[:],
            )
        mix = const.tile([P, 2, PACK], F32, name="mix")
        for u in range(HALVES):
            first_column = u * P * PAIR
            nc.vector.tensor_copy(
                out=mix[:, :, PAIR * u : PAIR * (u + 1)],
                in_=mix_t[:]
                .bitcast(BF16)[:, first_column : first_column + 2 * PAIR]
                .rearrange("q (c e) -> q c e", e=PAIR),
            )
        one_minus_mix = const.tile([P, 2, PACK], F32, name="one_minus_mix")
        nc.vector.tensor_scalar(
            out=one_minus_mix[:], in0=mix[:], scalar1=-1.0, scalar2=1.0, op0=ALU.mult, op1=ALU.add
        )

        w_grouped = const.tile([P, 2, A, PACK], BF16, name="w_grouped", align_bytes=64)
        for c in range(2):
            nc.vector.tensor_copy(out=w_grouped[:, c], in_=w_raw[:, c].rearrange("q t a -> q a t"))
        w_codes = const.tile([P, 2 * A], U32, name="w_codes", align_bytes=64)
        w_scales = const.tile([P, 2 * A], U8, name="w_scales", align_bytes=64)
        nc.vector.quantize_mx(
            out=w_codes[:].bitcast(FP8X4),
            scales=w_scales[:],
            in_=w_grouped[:].rearrange("q c a t -> q (c a t)"),
        )

        first_plus_decay = const.tile([P, A], F32, name="first_plus_decay")
        nc.vector.tensor_tensor(
            out=first_plus_decay[:], in0=first_bc[:], in1=decay_bc[:], op=ALU.add
        )
        two = const.tile([P, 1], F32, name="two")
        nc.vector.memset(two[:], 2.0)

        def over_tiles(row):
            return row[:].unsqueeze(1).to_broadcast([P, TILES, A])

        def twice(tile):
            return tile[:].unsqueeze(1).to_broadcast([P, 2, TILES, A])

        sab_all = const.tile([P, GROUPS, 2, TILES, A], BF16, name="sab_all")
        sp_all = const.tile([P, ROWS_PER_PARTITION, A], BF16, name="sp_all")

        live = {}

        def new(name, g, shape, dtype, bufs, pool=sbuf, align_bytes=None):
            live[name, g] = pool.tile(
                shape, dtype, name="%s_%d" % (name, g), tag=name, bufs=bufs, align_bytes=align_bytes
            )
            return live[name, g]

        def new_f32(name, g, bufs):
            return new(name, g, [P, TILES, A], F32, bufs)

        def new_f32_pair(name, g, bufs):
            return new(name, g, [P, 2, TILES, A], F32, bufs)

        def load(g):
            if not in_range(g):
                return
            nc.sync.dma_start(out=new("sx", g, [P, TILES, D], BF16, 2)[:], in_=sx_rows[:, rows_of(g), :])
            nc.sync.dma_start(out=new("x", g, [P, TILES, D], BF16, 2)[:], in_=x_rows[:, rows_of(g), :])
            nc.sync.dma_start(out=sp_all[:, rows_of(g), :], in_=sp_rows[:, rows_of(g), :])
            nc.sync.dma_start(out=sab_all[:, g, 1], in_=sb_rows[:, rows_of(g), :])
            nc.sync.dma_start(out=sab_all[:, g, 0], in_=sa_rows[:, rows_of(g), :])

        def transpose(name, g):
            if not in_range(g):
                return
            words = live[name, g][:].bitcast(F32)
            for u in range(HALVES):
                bank = new("%s_t%d" % (name, u), g, [P, GROUP], F32, 1, pool=psum)
                for j in range(TILES):
                    nc.tensor.transpose(
                        out=bank[:, j * P : (j + 1) * P],
                        in_=words[:, j, u * P : (u + 1) * P],
                        identity=identity[:],
                    )

        def value_of_word(name, g, t):
            u, e = divmod(t, PAIR)
            bank = live["%s_t%d" % (name, u), g]
            return bank[:].bitcast(BF16).rearrange("q (r e) -> q e r", e=PAIR)[:, e, :]

        def scale_saved_x(g):
            if not in_range(g):
                return
            scaled = new("scaled", g, [P, 2, PACK, GROUP], F32, 2)
            for t in range(PACK):
                for c in range(2):
                    nc.scalar.activation(
                        out=scaled[:, c, t, :],
                        in_=value_of_word("sx", g, t),
                        func=ACT.Copy,
                        scale=one_minus_mix[:, c, t : t + 1],
                    )

        def mix_x(g):
            if not in_range(g):
                return
            mixed = new("mixed", g, [P, 2, PACK, GROUP], BF16, 2)
            for t in range(PACK):
                for c in range(2):
                    nc.vector.scalar_tensor_tensor(
                        out=mixed[:, c, t, :],
                        in0=value_of_word("x", g, t),
                        scalar=mix[:, c, t : t + 1],
                        in1=live["scaled", g][:, c, t, :],
                        op0=ALU.mult,
                        op1=ALU.add,
                    )

        def group_words(g):
            if not in_range(g):
                return
            mixed = live["mixed", g]
            grouped = new("grouped", g, [P, 2, GROUP, PACK], BF16, 1, align_bytes=64)
            split = VECTOR_TILES * P
            nc.vector.tensor_copy(
                out=grouped[:, :, :split, :].rearrange("q c (n i) t -> q c n t i", i=4),
                in_=mixed[:, :, :, :split].rearrange("q c t (n i) -> q c n t i", i=4),
            )
            for c in range(2):
                nc.scalar.copy(
                    out=grouped[:, c, split:, :].rearrange("q (n i) t -> q n t i", i=4),
                    in_=mixed[:, c, :, split:].rearrange("q t (n i) -> q n t i", i=4),
                )

        def quantise(g):
            if not in_range(g):
                return
            codes = new("codes", g, [P, 2, GROUP], U32, 2, align_bytes=64)
            scales = new("scales", g, [P, 2, GROUP], U8, 2, align_bytes=64)
            nc.vector.quantize_mx(
                out=codes[:].rearrange("q c r -> q (c r)").bitcast(FP8X4),
                scales=scales[:].rearrange("q c r -> q (c r)"),
                in_=live["grouped", g][:].rearrange("q c r t -> q (c r t)"),
            )

        def project(g):
            if not in_range(g):
                return
            for c, (name, bufs) in enumerate((("k", 1), ("v", 3))):
                bank = new(name, g, [P, TILES, A], F32, bufs, pool=psum)
                for j in range(TILES):
                    tile_rows = slice(j * P, (j + 1) * P)
                    nc.tensor.matmul_mx(
                        out=bank[:, j, :],
                        lhsT=live["codes", g][:, c, tile_rows].bitcast(FP8X4),
                        lhsT_scale=live["scales", g][:, c, tile_rows],
                        rhs=w_codes[:, c * A : (c + 1) * A].bitcast(FP8X4),
                        rhs_scale=w_scales[:, c * A : (c + 1) * A],
                        start=True,
                        stop=True,
                    )

        def prepare_state(g):
            if not in_range(g):
                return
            nc.gpsimd.tensor_tensor(
                out=new_f32("w2", g, 2)[:], in0=sp_all[:, rows_of(g), :], in1=over_tiles(decay_bc), op=ALU.add
            )
            nc.gpsimd.tensor_scalar(
                out=new_f32_pair("factors", g, 3)[:, 0],
                in0=sab_all[:, g, 1],
                scalar1=-1.0,
                scalar2=1.0,
                op0=ALU.mult,
                op1=ALU.add,
            )

        def compare(g):
            if not in_range(g):
                return
            k, v, w2 = live["k", g], live["v", g], live["w2", g]
            nc.vector.tensor_tensor(out=new_f32("d2", g, 2)[:], in0=k[:], in1=w2[:], op=ALU.subtract)
            nc.vector.tensor_tensor(out=new_f32("p2", g, 2)[:], in0=k[:], in1=w2[:], op=ALU.max)
            nc.vector.tensor_tensor(out=live["factors", g][:, 1], in0=v[:], in1=sab_all[:, g, 0], op=ALU.subtract)
            nc.sync.dma_start(out=p2_rows[:, rows_of(g), :], in_=live["p2", g][:])
            nc.gpsimd.tensor_tensor(
                out=new_f32("d", g, 2)[:], in0=live["d2", g][:], in1=over_tiles(first_plus_decay), op=ALU.add
            )

        def exponentials(g):
            if not in_range(g):
                return
            d2, d = live["d2", g], live["d", g]
            nc.scalar.activation(out=new_f32("exp_up", g, 2)[:], in_=d2[:], func=ACT.Exp)
            nc.scalar.activation(out=new_f32("exp_down", g, 2)[:], in_=d2[:], func=ACT.Exp, scale=-1.0)
            nc.scalar.activation(out=new_f32("th", g, 2)[:], in_=d[:], func=ACT.Tanh, scale=0.5)

        def blend(g):
            if not in_range(g):
                return
            v, th, up, down = live["v", g], live["th", g], live["exp_up", g], live["exp_down", g]
            stt = nc.vector.scalar_tensor_tensor
            pulls = new_f32_pair("pulls", g, 2)
            f1_state = new_f32_pair("f1_state", g, 2)
            f2_v, num = new_f32("f2_v", g, 2), new_f32("num", g, 1)
            aa, bb = new_f32("aa", g, 2), new_f32("bb", g, 2)
            stt(out=pulls[:], in0=twice(th), scalar=1.0, in1=live["factors", g][:], op0=ALU.subtract, op1=ALU.mult)
            stt(out=f2_v[:], in0=up[:], scalar=1.0, in1=v[:], op0=ALU.min, op1=ALU.mult)
            stt(out=f1_state[:], in0=twice(down), scalar=1.0, in1=sab_all[:, g], op0=ALU.min, op1=ALU.mult)
            stt(out=num[:], in0=v[:], scalar=2.0, in1=pulls[:, 1], op0=ALU.mult, op1=ALU.add)
            stt(out=bb[:], in0=up[:], scalar=1.0, in1=f1_state[:, 1], op0=ALU.min, op1=ALU.add)
            stt(out=new_f32("num_den", g, LN_BATCH + 1)[:], in0=pulls[:, 0], scalar=2.0, in1=num[:], op0=ALU.add, op1=ALU.mult)
            nc.gpsimd.tensor_tensor(out=aa[:], in0=f1_state[:, 0], in1=f2_v[:], op=ALU.add)
            nc.sync.dma_start(out=aa_rows[:, rows_of(g), :], in_=aa[:])
            nc.sync.dma_start(out=bb_rows[:, rows_of(g), :], in_=bb[:])

        def square_den(g):
            if not in_range(g):
                return
            nc.scalar.activation(
                out=new_f32("inv_den2", g, LN_BATCH)[:], in_=live["pulls", g][:, 0], func=ACT.Square, bias=two[:, 0:1]
            )

        def invert_den2(last):
            if not (in_range(last) and ((last + 1) % LN_BATCH == 0 or last == GROUPS - 1)):
                return
            batch = range(last // LN_BATCH * LN_BATCH, last + 1)
            for g in batch:
                nc.scalar.activation(out=live["inv_den2", g][:], in_=live["inv_den2", g][:], func=ACT.Ln)
            for g in batch:
                nc.scalar.activation(out=live["inv_den2", g][:], in_=live["inv_den2", g][:], func=ACT.Exp, scale=-1.0)

        def divide(g, engine):
            if not in_range(g):
                return
            wkv = new_f32("wkv", g, LN_BATCH)
            engine.tensor_tensor(out=wkv[:], in0=live["num_den", g][:], in1=live["inv_den2", g][:], op=ALU.mult)
            nc.sync.dma_start(out=wkv_rows[:, rows_of(g), :], in_=wkv[:])

        for i in range(-2, GROUPS):
            load(i + 2)
            scale_saved_x(i)
            transpose("sx", i + 1)
            group_words(i - 1)
            blend(i - BLEND_LAG)
            compare(i - 2)
            divide(i - DIVIDE_LAG, nc.gpsimd)
            prepare_state(i - 1)
            mix_x(i)
            transpose("x", i + 1)
            quantise(i - 1)
            project(i - 1)
            square_den(i - BLEND_LAG)
            exponentials(i - 2)
            invert_den2(i - BLEND_LAG)
        for i in range(GROUPS, GROUPS + BLEND_LAG):
            group_words(i - 1)
            prepare_state(i - 1)
            compare(i - 2)
            divide(i - DIVIDE_LAG, nc.gpsimd)
            quantise(i - 1)
            project(i - 1)
            blend(i - BLEND_LAG)
            exponentials(i - 2)
            square_den(i - BLEND_LAG)
            invert_den2(i - BLEND_LAG)
        for g in range(GROUPS + BLEND_LAG - DIVIDE_LAG, GROUPS):
            divide(g, nc.vector)
